import numpy as np
import ml_dtypes


def mxq(x, axis, fmt="e4m3"):
    dtype, down = {"e4m3": (ml_dtypes.float8_e4m3fn, 7), "e5m2": (ml_dtypes.float8_e5m2, 14)}[fmt]
    v = np.moveaxis(np.asarray(x, np.float32).astype(ml_dtypes.bfloat16).astype(np.float64), axis, -1)
    blocks = v.reshape(v.shape[:-1] + (-1, 32))
    amax = np.abs(blocks).max(-1, keepdims=True)
    byte = np.maximum(np.where(amax > 0, np.frexp(amax)[1] - 1 + 127, 0) - down, 1)
    scale = np.exp2(byte - 127.0)
    codes = (blocks / scale).astype(np.float32).astype(dtype).astype(np.float64)
    return np.moveaxis((codes * scale).reshape(v.shape), -1, axis)


WIDE = False


def mx_kscale(k):
    if not WIDE:
        return np.ones(k)
    levels = np.array([10, -10, 5, -5, 0])
    a = np.random.permutation(np.resize(levels, k // 512 * 4)).reshape(k // 512, 4)
    idx = np.arange(k)
    return np.exp2(a[idx // 512, idx % 128 // 32])


BF16 = ml_dtypes.bfloat16


def bf(x):
    return np.asarray(x, np.float32).astype(BF16)


def f64(x):
    return np.asarray(x).astype(np.float64)


E2M1 = np.array([0.0, 0.5, 1.0, 1.5, 2.0, 3.0, 4.0, 6.0, -0.0, -0.5, -1.0, -1.5, -2.0, -3.0, -4.0, -6.0])


def pack_weight(w, fmt):
    k, n = w.shape
    w = f64(bf(w)).reshape(k // 32, 32, n)
    amax = np.abs(w).max(1)
    if fmt == "e4m3":
        byte = np.frexp(amax)[1] - 1 + 127 - 7
    else:
        mant, ex = np.frexp(amax / 6.0)
        byte = np.where(mant > 0.5, ex, ex - 1) + 127
    byte = np.clip(np.where(amax > 0, byte, 1), 1, 254)
    scaled = (w * np.exp2(127.0 - byte)[:, None, :]).reshape(k, n).astype(np.float32)
    by_word = np.ascontiguousarray(scaled.reshape(k // 512, 128, 4, n).transpose(0, 1, 3, 2))
    if fmt == "e4m3":
        words = by_word.astype(ml_dtypes.float8_e4m3fn).view(np.uint8)
    else:
        c = by_word.astype(ml_dtypes.float4_e2m1fn).view(np.uint8) & 0xF
        words = c[..., 0::2] | (c[..., 1::2] << 4)
    return np.ascontiguousarray(words), np.ascontiguousarray(byte.astype(np.uint8).reshape(k // 512, 16, n))


def unpack_weight(words, scales, fmt):
    g, p, n, _ = words.shape
    if fmt == "e4m3":
        vals = np.ascontiguousarray(words).view(ml_dtypes.float8_e4m3fn).astype(np.float64)
    else:
        nib = np.empty((g, p, n, 4), np.uint8)
        nib[..., 0::2] = words & 0xF
        nib[..., 1::2] = words >> 4
        vals = E2M1[nib]
    vals = vals * np.repeat(np.exp2(scales.astype(np.float64) - 127.0), 8, axis=1)[..., None]
    return vals.transpose(0, 1, 3, 2).reshape(g * 512, n)


B, S, D, HD, M = 2, 256, 16384, 128, 4
N = S // M
NEG = float(np.finfo(np.float32).min)
FMT = "e4m3"


def prev(x):
    return np.concatenate([np.zeros_like(x[:, :1]), x[:, :-1]], axis=1)


def setup_inputs():
    s = mx_kscale(D)

    def w():
        return pack_weight(np.random.standard_normal((D, HD)) / np.sqrt(D) / s[:, None], FMT)

    h = bf(np.random.standard_normal((B, S, D)) * s)
    w_kv_a_words, w_kv_a_scales = w()
    w_kv_b_words, w_kv_b_scales = w()
    w_z_a_words, w_z_a_scales = w()
    w_z_b_words, w_z_b_scales = w()
    b_a = bf(np.random.standard_normal((M, HD)) * 0.5)
    b_b = bf(np.random.standard_normal((M, HD)) * 0.5)
    return {"h": h,
            "w_kv_a_words": w_kv_a_words, "w_kv_a_scales": w_kv_a_scales,
            "w_kv_b_words": w_kv_b_words, "w_kv_b_scales": w_kv_b_scales,
            "w_z_a_words": w_z_a_words, "w_z_a_scales": w_z_a_scales,
            "w_z_b_words": w_z_b_words, "w_z_b_scales": w_z_b_scales,
            "b_a": b_a,
            "b_b": b_b}


def reference(h, w_kv_a_words, w_kv_a_scales, w_kv_b_words, w_kv_b_scales, w_z_a_words, w_z_a_scales, w_z_b_words, w_z_b_scales, b_a, b_b):
    hq = mxq(f64(h), 2, "e4m3")
    c_a = (hq @ unpack_weight(w_kv_a_words, w_kv_a_scales, FMT)).reshape(B, N, M, HD)
    c_b = (hq @ unpack_weight(w_kv_b_words, w_kv_b_scales, FMT)).reshape(B, N, M, HD)
    z_a = (hq @ unpack_weight(w_z_a_words, w_z_a_scales, FMT)).reshape(B, N, M, HD)
    z_b = (hq @ unpack_weight(w_z_b_words, w_z_b_scales, FMT)).reshape(B, N, M, HD)
    logits = np.concatenate([prev(z_b) + f64(b_b), z_a + f64(b_a)], axis=2)
    valid = np.concatenate([np.broadcast_to((np.arange(N) > 0)[:, None], (N, M)), np.ones((N, M), bool)], axis=1)
    logits = np.where(valid[None, :, :, None], logits, NEG)
    e = np.exp(logits - logits.max(axis=2, keepdims=True))
    weights = e / e.sum(axis=2, keepdims=True)
    c_vals = np.concatenate([prev(c_b), c_a], axis=2)
    return np.sum(weights * c_vals, axis=2)

@@ -1,0 +1,244 @@
+from contextlib import ExitStack
+
+import concourse.mybir as mybir
+from concourse.masks import make_identity
+
+F32 = mybir.dt.float32
+BF16 = mybir.dt.bfloat16
+I32 = mybir.dt.int32
+U32 = mybir.dt.uint32
+U8 = mybir.dt.uint8
+FP8X4 = mybir.dt.float8_e4m3fn_x4
+ALU = mybir.AluOpType
+ACT = mybir.ActivationFunctionType
+AXIS = mybir.AxisListType
+
+P = 128
+PACK = 4
+K_PASS = P * PACK
+BATCH, SEQ, DIM, FEAT, BLOCK = 2, 256, 16384, 128, 4
+TOKENS = BATCH * SEQ
+TOKEN_TILES = TOKENS // P
+GROUPS = DIM // K_PASS
+BLOCKS = SEQ // BLOCK
+WINDOW = 2 * BLOCK
+PAIRS = K_PASS // 2
+
+CHUNK_GROUPS = 4
+CHUNKS = GROUPS // CHUNK_GROUPS
+CHUNK_K = CHUNK_GROUPS * K_PASS
+RAW_BUFS = 3
+ROUND_GROUPS = 2
+ROUNDS = GROUPS // ROUND_GROUPS
+ROUNDS_PER_CHUNK = CHUNK_GROUPS // ROUND_GROUPS
+
+LOGITS = ("z_a", "z_b")
+VALUES = ("c_b", "c_a")
+PROJECTIONS = LOGITS + VALUES
+NEG = -3.4028234663852886e38
+
+FLOPS = 2 * TOKENS * DIM * len(PROJECTIONS) * FEAT
+
+
+def tile_tokenlevelcompressor_pa_k_kernel(
+    tc,
+    h,
+    w_kv_a_words,
+    w_kv_a_scales,
+    w_kv_b_words,
+    w_kv_b_scales,
+    w_z_a_words,
+    w_z_a_scales,
+    w_z_b_words,
+    w_z_b_scales,
+    b_a,
+    b_b,
+    out,
+):
+    nc = tc.nc
+    h_rows = h.rearrange("b s d -> (b s) d")
+    words_in = {"z_a": w_z_a_words, "z_b": w_z_b_words, "c_b": w_kv_b_words, "c_a": w_kv_a_words}
+    scales_in = {"z_a": w_z_a_scales, "z_b": w_z_b_scales, "c_b": w_kv_b_scales, "c_a": w_kv_a_scales}
+    plane_start = {name: PACK * i for i, name in enumerate(PROJECTIONS)}
+
+    with ExitStack() as ctx:
+        ctx.enter_context(tc.manual_schedule())
+        keep = ctx.enter_context(tc.tile_pool(name="keep", bufs=1))
+        psum_acc = ctx.enter_context(tc.psum_pool(name="psum_acc", bufs=1))
+        psum_tr = ctx.enter_context(tc.psum_pool(name="psum_tr", bufs=4))
+
+        w_words = {n: keep.tile([P, GROUPS, FEAT], I32, name="w_words_" + n, align_bytes=64) for n in PROJECTIONS}
+        w_planes = keep.tile([P, GROUPS, FEAT], U8, name="w_planes", align_bytes=64)
+        h_codes = keep.tile([P, GROUPS, TOKENS], U32, name="h_codes", align_bytes=64)
+        h_planes = keep.tile([P, GROUPS, TOKENS], U8, name="h_planes", align_bytes=64)
+        acc = {n: psum_acc.tile([P, TOKENS], F32, name="acc_" + n) for n in PROJECTIONS}
+
+        def load_words(name, c):
+            groups = slice(c * CHUNK_GROUPS, (c + 1) * CHUNK_GROUPS)
+            nc.sync.dma_start(
+                out=w_words[name][:, groups, :],
+                in_=words_in[name][groups].rearrange("g p n t -> p g (n t)").bitcast(I32),
+            )
+
+        def mx_pass(name, g):
+            nc.tensor.matmul_mx(
+                out=acc[name][:],
+                lhsT=w_words[name][:, g, :].bitcast(FP8X4),
+                lhsT_scale=w_planes[plane_start[name] : P, g, :],
+                rhs=h_codes[:, g, :].bitcast(FP8X4),
+                rhs_scale=h_planes[:, g, :],
+                start=(g == 0),
+                stop=(g == GROUPS - 1),
+            )
+
+        ident = keep.tile([P, P], F32, name="ident")
+        make_identity(nc, ident[:])
+        nc.vector.memset(w_planes[:].rearrange("p g n -> p (g n)").bitcast(I32), 0)
+        bias_rows_bf = keep.tile([P, P], BF16, name="bias_rows_bf")
+        nc.vector.memset(bias_rows_bf[:], 0.0)
+        nc.scalar.dma_start(out=bias_rows_bf[0:BLOCK, :], in_=b_b)
+        nc.scalar.dma_start(out=bias_rows_bf[BLOCK:WINDOW, :], in_=b_a)
+        bias_rows = keep.tile([P, P], F32, name="bias_rows")
+        nc.vector.tensor_copy(out=bias_rows[:], in_=bias_rows_bf[:])
+        bias_bank = psum_tr.tile([P, 2, 2 * P], F32, name="bank")
+        nc.tensor.transpose(bias_bank[:, 0, 0:P], bias_rows[:], ident[:])
+        bias = keep.tile([P, WINDOW], F32, name="bias")
+        nc.scalar.copy(out=bias[:], in_=bias_bank[:, 0, 0:WINDOW])
+
+        with tc.tile_pool(name="raw", bufs=RAW_BUFS) as raw_pool, tc.tile_pool(name="grouped", bufs=4) as grouped_pool:
+            raw_of = {}
+            grouped_of = {}
+
+            def load_chunk(c):
+                raw = raw_pool.tile([P, TOKEN_TILES, CHUNK_K], BF16, name="raw")
+                for t in range(TOKEN_TILES):
+                    nc.sync.dma_start(out=raw[:, t, :], in_=h_rows[t * P : (t + 1) * P, c * CHUNK_K : (c + 1) * CHUNK_K])
+                raw_of[c] = raw
+                for name in LOGITS:
+                    load_words(name, c)
+
+            def transpose_round(r):
+                for g in range(r * ROUND_GROUPS, (r + 1) * ROUND_GROUPS):
+                    raw_words = raw_of[g // CHUNK_GROUPS][:].bitcast(F32)
+                    first = (g % CHUNK_GROUPS) * PAIRS
+                    grouped = grouped_pool.tile([P, TOKENS * PACK], BF16, name="grouped", align_bytes=64)
+                    grouped_words = grouped[:].bitcast(F32).rearrange("p (r u) -> p r u", u=2)
+                    for half in range(2):
+                        bank = psum_tr.tile([P, 2, 2 * P], F32, name="bank")
+                        for t in range(2):
+                            for u in range(2):
+                                nc.tensor.transpose(
+                                    bank[:, u, t * P : (t + 1) * P],
+                                    raw_words[:, 2 * half + t, first + u : first + PAIRS : 2],
+                                    ident[:],
+                                )
+                        nc.scalar.copy(
+                            out=grouped_words[:, half * 2 * P : (half + 1) * 2 * P, :],
+                            in_=bank[:].rearrange("p u r -> p r u"),
+                        )
+                    grouped_of[g] = grouped
+                c = r // ROUNDS_PER_CHUNK
+                if r % ROUNDS_PER_CHUNK == ROUNDS_PER_CHUNK - 1 and c + RAW_BUFS < CHUNKS:
+                    load_chunk(c + RAW_BUFS)
+
+            def quantise_round(r):
+                for g in range(r * ROUND_GROUPS, (r + 1) * ROUND_GROUPS):
+                    nc.vector.quantize_mx(
+                        out=h_codes[:, g, :].bitcast(FP8X4), scales=h_planes[:, g, :], in_=grouped_of[g][:]
+                    )
+
+            load_chunk(0)
+            for name in PROJECTIONS:
+                rows = scales_in[name].rearrange("g q n -> q g n").bitcast(I32)
+                for quad in range(4):
+                    top = 32 * quad + plane_start[name]
+                    nc.sync.dma_start(
+                        out=w_planes[top : top + PACK, :, :].bitcast(I32), in_=rows[PACK * quad : PACK * (quad + 1)]
+                    )
+            for c in range(1, RAW_BUFS):
+                load_chunk(c)
+
+            transpose_round(0)
+            for r in range(ROUNDS):
+                quantise_round(r)
+                if r + 1 < ROUNDS:
+                    transpose_round(r + 1)
+                for g in range(r * ROUND_GROUPS, (r + 1) * ROUND_GROUPS):
+                    for name in LOGITS:
+                        mx_pass(name, g)
+
+        for name in VALUES:
+            for c in range(CHUNKS):
+                load_words(name, c)
+
+        soft = ctx.enter_context(tc.tile_pool(name="soft", bufs=1))
+
+        def by_block(ap):
+            return ap.rearrange("p (n j i) -> p n j i", n=BATCH, i=BLOCK)
+
+        def flat(ap):
+            return ap.rearrange("p n j e -> p (n j) e")
+
+        window = soft.tile([P, BATCH, BLOCKS, WINDOW], F32, name="window")
+        nc.vector.memset(window[:, :, 0:1, 0:BLOCK], NEG)
+        nc.vector.tensor_tensor(
+            out=window[:, :, 1:BLOCKS, 0:BLOCK],
+            in0=by_block(acc["z_b"][:])[:, :, 0 : BLOCKS - 1, :],
+            in1=bias[:, 0:BLOCK].unsqueeze(1).unsqueeze(1).to_broadcast([P, BATCH, BLOCKS - 1, BLOCK]),
+            op=ALU.add,
+        )
+        nc.vector.tensor_tensor(
+            out=window[:, :, :, BLOCK:WINDOW],
+            in0=by_block(acc["z_a"][:]),
+            in1=bias[:, BLOCK:WINDOW].unsqueeze(1).unsqueeze(1).to_broadcast([P, BATCH, BLOCKS, BLOCK]),
+            op=ALU.add,
+        )
+        top_logit = soft.tile([P, BATCH * BLOCKS], F32, name="top_logit")
+        nc.vector.tensor_reduce(out=top_logit[:], in_=flat(window[:]), axis=AXIS.X, op=ALU.max)
+        nc.vector.tensor_tensor(
+            out=flat(window[:]),
+            in0=flat(window[:]),
+            in1=top_logit[:].unsqueeze(2).to_broadcast([P, BATCH * BLOCKS, WINDOW]),
+            op=ALU.subtract,
+        )
+        weight = soft.tile([P, BATCH, BLOCKS, WINDOW], F32, name="weight")
+        nc.scalar.activation(out=flat(weight[:]), in_=flat(window[:]), func=ACT.Exp)
+        total = soft.tile([P, BATCH * BLOCKS], F32, name="total")
+        nc.vector.tensor_reduce(out=total[:], in_=flat(weight[:]), axis=AXIS.X, op=ALU.add)
+        inverse = soft.tile([P, BATCH * BLOCKS], F32, name="inverse")
+        nc.vector.reciprocal(out=inverse[:], in_=total[:])
+        nc.vector.tensor_tensor(
+            out=flat(weight[:]),
+            in0=flat(weight[:]),
+            in1=inverse[:].unsqueeze(2).to_broadcast([P, BATCH * BLOCKS, WINDOW]),
+            op=ALU.mult,
+        )
+
+        for g in range(GROUPS):
+            mx_pass("c_b", g)
+        part_b = soft.tile([P, BATCH, BLOCKS, BLOCK], F32, name="part_b")
+        nc.vector.memset(part_b[:, :, 0:1, :], 0.0)
+        nc.vector.tensor_tensor(
+            out=part_b[:, :, 1:BLOCKS, :],
+            in0=weight[:, :, 1:BLOCKS, 0:BLOCK],
+            in1=by_block(acc["c_b"][:])[:, :, 0 : BLOCKS - 1, :],
+            op=ALU.mult,
+        )
+        sum_b = soft.tile([P, BATCH * BLOCKS], F32, name="sum_b")
+        nc.vector.tensor_reduce(out=sum_b[:], in_=flat(part_b[:]), axis=AXIS.X, op=ALU.add)
+
+        for g in range(GROUPS):
+            mx_pass("c_a", g)
+        part_a = soft.tile([P, BATCH, BLOCKS, BLOCK], F32, name="part_a")
+        nc.vector.tensor_tensor(
+            out=part_a[:], in0=weight[:, :, :, BLOCK:WINDOW], in1=by_block(acc["c_a"][:]), op=ALU.mult
+        )
+        result = soft.tile([P, BATCH * BLOCKS], F32, name="result")
+        nc.vector.tensor_reduce(out=result[:], in_=flat(part_a[:]), axis=AXIS.X, op=ALU.add)
+        nc.vector.tensor_tensor(out=result[:], in0=result[:], in1=sum_b[:], op=ALU.add)
+
+        result_bank = psum_tr.tile([P, 2, 2 * P], F32, name="bank")
+        nc.tensor.transpose(result_bank[:, 0, 0:P], result[:], ident[:])
+        result_rows = soft.tile([P, FEAT], F32, name="result_rows")
+        nc.vector.tensor_copy(out=result_rows[:], in_=result_bank[:, 0, 0:P])
+        nc.sync.dma_start(out=out.rearrange("n j f -> (n j) f"), in_=result_rows[:])

@@ -105,8 +105,11 @@ def tile_tokenlevelcompressor_pa_k_kernel(
         bias = keep.tile([P, WINDOW], F32, name="bias")
         nc.scalar.copy(out=bias[:], in_=bias_bank[:, 0, 0:WINDOW])
 
-        with tc.tile_pool(name="raw", bufs=RAW_BUFS) as raw_pool, tc.tile_pool(name="grouped", bufs=4) as grouped_pool:
+        with tc.tile_pool(name="raw", bufs=RAW_BUFS) as raw_pool, tc.tile_pool(
+            name="sorted", bufs=2 * ROUND_GROUPS
+        ) as sorted_pool, tc.tile_pool(name="grouped", bufs=2 * ROUND_GROUPS) as grouped_pool:
             raw_of = {}
+            sorted_of = {}
             grouped_of = {}
 
             def load_chunk(c):
@@ -117,10 +120,22 @@ def tile_tokenlevelcompressor_pa_k_kernel(
                 for name in LOGITS:
                     load_words(name, c)
 
-            def transpose_round(r):
+            def sort_round(r):
                 for g in range(r * ROUND_GROUPS, (r + 1) * ROUND_GROUPS):
                     raw_words = raw_of[g // CHUNK_GROUPS][:].bitcast(F32)
                     first = (g % CHUNK_GROUPS) * PAIRS
+                    sorted_words = sorted_pool.tile([P, TOKEN_TILES, 2, P], F32, name="sorted_words")
+                    nc.vector.tensor_copy(
+                        out=sorted_words[:],
+                        in_=raw_words[:, :, first : first + PAIRS].rearrange("p t (q u) -> p t u q", u=2),
+                    )
+                    sorted_of[g] = sorted_words
+                c = r // ROUNDS_PER_CHUNK
+                if r % ROUNDS_PER_CHUNK == ROUNDS_PER_CHUNK - 1 and c + RAW_BUFS < CHUNKS:
+                    load_chunk(c + RAW_BUFS)
+
+            def transpose_round(r):
+                for g in range(r * ROUND_GROUPS, (r + 1) * ROUND_GROUPS):
                     grouped = grouped_pool.tile([P, TOKENS * PACK], BF16, name="grouped", align_bytes=64)
                     grouped_words = grouped[:].bitcast(F32).rearrange("p (r u) -> p r u", u=2)
                     for half in range(2):
@@ -129,7 +144,7 @@ def tile_tokenlevelcompressor_pa_k_kernel(
                             for u in range(2):
                                 nc.tensor.transpose(
                                     bank[:, u, t * P : (t + 1) * P],
-                                    raw_words[:, 2 * half + t, first + u : first + PAIRS : 2],
+                                    sorted_of[g][:, 2 * half + t, u, :],
                                     ident[:],
                                 )
                         nc.scalar.copy(
@@ -137,9 +152,6 @@ def tile_tokenlevelcompressor_pa_k_kernel(
                             in_=bank[:].rearrange("p u r -> p r u"),
                         )
                     grouped_of[g] = grouped
-                c = r // ROUNDS_PER_CHUNK
-                if r % ROUNDS_PER_CHUNK == ROUNDS_PER_CHUNK - 1 and c + RAW_BUFS < CHUNKS:
-                    load_chunk(c + RAW_BUFS)
 
             def quantise_round(r):
                 for g in range(r * ROUND_GROUPS, (r + 1) * ROUND_GROUPS):
@@ -158,9 +170,13 @@ def tile_tokenlevelcompressor_pa_k_kernel(
             for c in range(1, RAW_BUFS):
                 load_chunk(c)
 
+            sort_round(0)
+            sort_round(1)
             transpose_round(0)
             for r in range(ROUNDS):
                 quantise_round(r)
+                if r + 2 < ROUNDS:
+                    sort_round(r + 2)
                 if r + 1 < ROUNDS:
                     transpose_round(r + 1)
                 for g in range(r * ROUND_GROUPS, (r + 1) * ROUND_GROUPS):

@@ -28,6 +28,7 @@ CHUNK_GROUPS = 4
 CHUNKS = GROUPS // CHUNK_GROUPS
 CHUNK_K = CHUNK_GROUPS * K_PASS
 RAW_BUFS = 3
+DEFER_GROUPS = 12
 ROUND_GROUPS = 2
 ROUNDS = GROUPS // ROUND_GROUPS
 ROUNDS_PER_CHUNK = CHUNK_GROUPS // ROUND_GROUPS
@@ -100,10 +101,12 @@ def tile_tokenlevelcompressor_pa_k_kernel(
         nc.scalar.dma_start(out=bias_rows_bf[BLOCK:WINDOW, :], in_=b_a)
         bias_rows = keep.tile([P, P], F32, name="bias_rows")
         nc.vector.tensor_copy(out=bias_rows[:], in_=bias_rows_bf[:])
-        bias_bank = psum_tr.tile([P, 2, 2 * P], F32, name="bank")
-        nc.tensor.transpose(bias_bank[:, 0, 0:P], bias_rows[:], ident[:])
         bias = keep.tile([P, WINDOW], F32, name="bias")
-        nc.scalar.copy(out=bias[:], in_=bias_bank[:, 0, 0:WINDOW])
+
+        def transpose_bias():
+            bias_bank = psum_tr.tile([P, 2, 2 * P], F32, name="bank")
+            nc.tensor.transpose(bias_bank[:, 0, 0:P], bias_rows[:], ident[:])
+            nc.scalar.copy(out=bias[:], in_=bias_bank[:, 0, 0:WINDOW])
 
         with tc.tile_pool(name="raw", bufs=RAW_BUFS) as raw_pool, tc.tile_pool(
             name="sorted", bufs=2 * ROUND_GROUPS
@@ -114,11 +117,18 @@ def tile_tokenlevelcompressor_pa_k_kernel(
 
             def load_chunk(c):
                 raw = raw_pool.tile([P, TOKEN_TILES, CHUNK_K], BF16, name="raw")
-                for t in range(TOKEN_TILES):
-                    nc.sync.dma_start(out=raw[:, t, :], in_=h_rows[t * P : (t + 1) * P, c * CHUNK_K : (c + 1) * CHUNK_K])
+                step = K_PASS if c == 0 else CHUNK_K
+                for k in range(0, CHUNK_K, step):
+                    nc.sync.dma_start(
+                        out=raw[:, :, k : k + step],
+                        in_=h_rows[:, c * CHUNK_K + k : c * CHUNK_K + k + step].rearrange("(t p) k -> p t k", p=P),
+                    )
                 raw_of[c] = raw
                 for name in LOGITS:
                     load_words(name, c)
+                if c < CHUNKS - DEFER_GROUPS // CHUNK_GROUPS:
+                    for name in VALUES:
+                        load_words(name, c)
 
             def sort_round(r):
                 for g in range(r * ROUND_GROUPS, (r + 1) * ROUND_GROUPS):
@@ -179,12 +189,14 @@ def tile_tokenlevelcompressor_pa_k_kernel(
                     sort_round(r + 2)
                 if r + 1 < ROUNDS:
                     transpose_round(r + 1)
+                else:
+                    transpose_bias()
                 for g in range(r * ROUND_GROUPS, (r + 1) * ROUND_GROUPS):
-                    for name in LOGITS:
+                    for name in PROJECTIONS if g < GROUPS - DEFER_GROUPS else LOGITS:
                         mx_pass(name, g)
 
         for name in VALUES:
-            for c in range(CHUNKS):
+            for c in range(CHUNKS - DEFER_GROUPS // CHUNK_GROUPS, CHUNKS):
                 load_words(name, c)
 
         soft = ctx.enter_context(tc.tile_pool(name="soft", bufs=1))
@@ -223,14 +235,8 @@ def tile_tokenlevelcompressor_pa_k_kernel(
         nc.vector.tensor_reduce(out=total[:], in_=flat(weight[:]), axis=AXIS.X, op=ALU.add)
         inverse = soft.tile([P, BATCH * BLOCKS], F32, name="inverse")
         nc.vector.reciprocal(out=inverse[:], in_=total[:])
-        nc.vector.tensor_tensor(
-            out=flat(weight[:]),
-            in0=flat(weight[:]),
-            in1=inverse[:].unsqueeze(2).to_broadcast([P, BATCH * BLOCKS, WINDOW]),
-            op=ALU.mult,
-        )
 
-        for g in range(GROUPS):
+        for g in range(GROUPS - DEFER_GROUPS, GROUPS):
             mx_pass("c_b", g)
         part_b = soft.tile([P, BATCH, BLOCKS, BLOCK], F32, name="part_b")
         nc.vector.memset(part_b[:, :, 0:1, :], 0.0)
@@ -243,7 +249,7 @@ def tile_tokenlevelcompressor_pa_k_kernel(
         sum_b = soft.tile([P, BATCH * BLOCKS], F32, name="sum_b")
         nc.vector.tensor_reduce(out=sum_b[:], in_=flat(part_b[:]), axis=AXIS.X, op=ALU.add)
 
-        for g in range(GROUPS):
+        for g in range(GROUPS - DEFER_GROUPS, GROUPS):
             mx_pass("c_a", g)
         part_a = soft.tile([P, BATCH, BLOCKS, BLOCK], F32, name="part_a")
         nc.vector.tensor_tensor(
@@ -252,6 +258,7 @@ def tile_tokenlevelcompressor_pa_k_kernel(
         result = soft.tile([P, BATCH * BLOCKS], F32, name="result")
         nc.vector.tensor_reduce(out=result[:], in_=flat(part_a[:]), axis=AXIS.X, op=ALU.add)
         nc.vector.tensor_tensor(out=result[:], in0=result[:], in1=sum_b[:], op=ALU.add)
+        nc.vector.tensor_tensor(out=result[:], in0=result[:], in1=inverse[:], op=ALU.mult)
 
         result_bank = psum_tr.tile([P, 2, 2 * P], F32, name="bank")
         nc.tensor.transpose(result_bank[:, 0, 0:P], result[:], ident[:])

@@ -172,10 +172,9 @@ def tile_tokenlevelcompressor_pa_k_kernel(
             load_chunk(0)
             for name in PROJECTIONS:
                 rows = scales_in[name].rearrange("g q n -> q g n").bitcast(I32)
-                for quad in range(4):
-                    top = 32 * quad + plane_start[name]
+                for s in range(PACK):
                     nc.sync.dma_start(
-                        out=w_planes[top : top + PACK, :, :].bitcast(I32), in_=rows[PACK * quad : PACK * (quad + 1)]
+                        out=w_planes[plane_start[name] + s : P : 32, :, :].bitcast(I32), in_=rows[s : 4 * PACK : PACK]
                     )
             for c in range(1, RAW_BUFS):
                 load_chunk(c)

@@ -22,13 +22,13 @@ TOKEN_TILES = TOKENS // P
 GROUPS = DIM // K_PASS
 BLOCKS = SEQ // BLOCK
 WINDOW = 2 * BLOCK
+GROUP_BLOCKS = K_PASS // 32
 PAIRS = K_PASS // 2
 
 CHUNK_GROUPS = 4
 CHUNKS = GROUPS // CHUNK_GROUPS
 CHUNK_K = CHUNK_GROUPS * K_PASS
 RAW_BUFS = 3
-DEFER_GROUPS = 12
 ROUND_GROUPS = 2
 ROUNDS = GROUPS // ROUND_GROUPS
 ROUNDS_PER_CHUNK = CHUNK_GROUPS // ROUND_GROUPS
@@ -36,6 +36,9 @@ ROUNDS_PER_CHUNK = CHUNK_GROUPS // ROUND_GROUPS
 LOGITS = ("z_a", "z_b")
 VALUES = ("c_b", "c_a")
 PROJECTIONS = LOGITS + VALUES
+STREAMED = LOGITS + ("c_b",)
+FIRST_SPLIT = 2
+BIAS_CHUNK = 2
 NEG = -3.4028234663852886e38
 
 FLOPS = 2 * TOKENS * DIM * len(PROJECTIONS) * FEAT
@@ -60,7 +63,7 @@ def tile_tokenlevelcompressor_pa_k_kernel(
     h_rows = h.rearrange("b s d -> (b s) d")
     words_in = {"z_a": w_z_a_words, "z_b": w_z_b_words, "c_b": w_kv_b_words, "c_a": w_kv_a_words}
     scales_in = {"z_a": w_z_a_scales, "z_b": w_z_b_scales, "c_b": w_kv_b_scales, "c_a": w_kv_a_scales}
-    plane_start = {name: PACK * i for i, name in enumerate(PROJECTIONS)}
+    plane_start = {"z_a": 0, "z_b": PACK, "c_b": 0, "c_a": 0}
 
     with ExitStack() as ctx:
         ctx.enter_context(tc.manual_schedule())
@@ -69,7 +72,10 @@ def tile_tokenlevelcompressor_pa_k_kernel(
         psum_tr = ctx.enter_context(tc.psum_pool(name="psum_tr", bufs=4))
 
         w_words = {n: keep.tile([P, GROUPS, FEAT], I32, name="w_words_" + n, align_bytes=64) for n in PROJECTIONS}
-        w_planes = keep.tile([P, GROUPS, FEAT], U8, name="w_planes", align_bytes=64)
+        logit_planes = keep.tile([P, GROUPS, FEAT], U8, name="logit_planes", align_bytes=64)
+        w_planes = {n: logit_planes for n in LOGITS}
+        for n in VALUES:
+            w_planes[n] = keep.tile([P, GROUPS, FEAT], U8, name="planes_" + n, align_bytes=64)
         h_codes = keep.tile([P, GROUPS, TOKENS], U32, name="h_codes", align_bytes=64)
         h_planes = keep.tile([P, GROUPS, TOKENS], U8, name="h_planes", align_bytes=64)
         acc = {n: psum_acc.tile([P, TOKENS], F32, name="acc_" + n) for n in PROJECTIONS}
@@ -81,11 +87,19 @@ def tile_tokenlevelcompressor_pa_k_kernel(
                 in_=words_in[name][groups].rearrange("g p n t -> p g (n t)").bitcast(I32),
             )
 
+        def load_scales(name):
+            rows = scales_in[name].rearrange("g q n -> q g n").bitcast(I32)
+            for s in range(PACK):
+                nc.sync.dma_start(
+                    out=w_planes[name][plane_start[name] + s : P : 32, :, :].bitcast(I32),
+                    in_=rows[s : GROUP_BLOCKS : PACK],
+                )
+
         def mx_pass(name, g):
             nc.tensor.matmul_mx(
                 out=acc[name][:],
                 lhsT=w_words[name][:, g, :].bitcast(FP8X4),
-                lhsT_scale=w_planes[plane_start[name] : P, g, :],
+                lhsT_scale=w_planes[name][plane_start[name] : P, g, :],
                 rhs=h_codes[:, g, :].bitcast(FP8X4),
                 rhs_scale=h_planes[:, g, :],
                 start=(g == 0),
@@ -94,14 +108,16 @@ def tile_tokenlevelcompressor_pa_k_kernel(
 
         ident = keep.tile([P, P], F32, name="ident")
         make_identity(nc, ident[:])
-        nc.vector.memset(w_planes[:].rearrange("p g n -> p (g n)").bitcast(I32), 0)
+        for planes in (logit_planes, w_planes["c_b"], w_planes["c_a"]):
+            nc.vector.memset(planes[:].rearrange("p g n -> p (g n)").bitcast(I32), 0)
         bias_rows_bf = keep.tile([P, P], BF16, name="bias_rows_bf")
         nc.vector.memset(bias_rows_bf[:], 0.0)
-        nc.scalar.dma_start(out=bias_rows_bf[0:BLOCK, :], in_=b_b)
-        nc.scalar.dma_start(out=bias_rows_bf[BLOCK:WINDOW, :], in_=b_a)
         bias_rows = keep.tile([P, P], F32, name="bias_rows")
-        nc.vector.tensor_copy(out=bias_rows[:], in_=bias_rows_bf[:])
         bias = keep.tile([P, WINDOW], F32, name="bias")
+
+        def load_bias():
+            nc.sync.dma_start(out=bias_rows_bf[0:BLOCK, :], in_=b_b)
+            nc.sync.dma_start(out=bias_rows_bf[BLOCK:WINDOW, :], in_=b_a)
 
         def transpose_bias():
             bias_bank = psum_tr.tile([P, 2, 2 * P], F32, name="bank")
@@ -110,25 +126,31 @@ def tile_tokenlevelcompressor_pa_k_kernel(
 
         with tc.tile_pool(name="raw", bufs=RAW_BUFS) as raw_pool, tc.tile_pool(
             name="sorted", bufs=2 * ROUND_GROUPS
-        ) as sorted_pool, tc.tile_pool(name="grouped", bufs=2 * ROUND_GROUPS) as grouped_pool:
+        ) as sorted_pool, tc.tile_pool(name="grouped", bufs=3) as grouped_pool:
             raw_of = {}
             sorted_of = {}
             grouped_of = {}
 
-            def load_chunk(c):
+            def load_h(c):
                 raw = raw_pool.tile([P, TOKEN_TILES, CHUNK_K], BF16, name="raw")
-                step = K_PASS if c == 0 else CHUNK_K
+                step = FIRST_SPLIT * K_PASS if c == 0 else CHUNK_K
                 for k in range(0, CHUNK_K, step):
                     nc.sync.dma_start(
                         out=raw[:, :, k : k + step],
                         in_=h_rows[:, c * CHUNK_K + k : c * CHUNK_K + k + step].rearrange("(t p) k -> p t k", p=P),
                     )
                 raw_of[c] = raw
-                for name in LOGITS:
+
+            def load_chunk(c):
+                load_h(c)
+                for name in STREAMED:
                     load_words(name, c)
-                if c < CHUNKS - DEFER_GROUPS // CHUNK_GROUPS:
-                    for name in VALUES:
-                        load_words(name, c)
+                if c == BIAS_CHUNK:
+                    load_bias()
+                if c == CHUNKS - 1:
+                    load_scales("c_a")
+                    for other in range(CHUNKS):
+                        load_words("c_a", other)
 
             def sort_round(r):
                 for g in range(r * ROUND_GROUPS, (r + 1) * ROUND_GROUPS):
@@ -169,13 +191,13 @@ def tile_tokenlevelcompressor_pa_k_kernel(
                         out=h_codes[:, g, :].bitcast(FP8X4), scales=h_planes[:, g, :], in_=grouped_of[g][:]
                     )
 
-            load_chunk(0)
-            for name in PROJECTIONS:
-                rows = scales_in[name].rearrange("g q n -> q g n").bitcast(I32)
-                for s in range(PACK):
-                    nc.sync.dma_start(
-                        out=w_planes[plane_start[name] + s : P : 32, :, :].bitcast(I32), in_=rows[s : 4 * PACK : PACK]
-                    )
+            load_h(0)
+            for name in LOGITS:
+                load_scales(name)
+            for name in LOGITS:
+                load_words(name, 0)
+            load_scales("c_b")
+            load_words("c_b", 0)
             for c in range(1, RAW_BUFS):
                 load_chunk(c)
 
@@ -183,20 +205,18 @@ def tile_tokenlevelcompressor_pa_k_kernel(
             sort_round(1)
             transpose_round(0)
             for r in range(ROUNDS):
+                if r == ROUNDS - 2:
+                    nc.vector.tensor_copy(out=bias_rows[:], in_=bias_rows_bf[:])
                 quantise_round(r)
                 if r + 2 < ROUNDS:
                     sort_round(r + 2)
                 if r + 1 < ROUNDS:
                     transpose_round(r + 1)
-                else:
+                if r == ROUNDS - 2:
                     transpose_bias()
                 for g in range(r * ROUND_GROUPS, (r + 1) * ROUND_GROUPS):
-                    for name in PROJECTIONS if g < GROUPS - DEFER_GROUPS else LOGITS:
+                    for name in STREAMED:
                         mx_pass(name, g)
-
-        for name in VALUES:
-            for c in range(CHUNKS - DEFER_GROUPS // CHUNK_GROUPS, CHUNKS):
-                load_words(name, c)
 
         soft = ctx.enter_context(tc.tile_pool(name="soft", bufs=1))
 
@@ -235,8 +255,6 @@ def tile_tokenlevelcompressor_pa_k_kernel(
         inverse = soft.tile([P, BATCH * BLOCKS], F32, name="inverse")
         nc.vector.reciprocal(out=inverse[:], in_=total[:])
 
-        for g in range(GROUPS - DEFER_GROUPS, GROUPS):
-            mx_pass("c_b", g)
         part_b = soft.tile([P, BATCH, BLOCKS, BLOCK], F32, name="part_b")
         nc.vector.memset(part_b[:, :, 0:1, :], 0.0)
         nc.vector.tensor_tensor(
@@ -248,7 +266,7 @@ def tile_tokenlevelcompressor_pa_k_kernel(
         sum_b = soft.tile([P, BATCH * BLOCKS], F32, name="sum_b")
         nc.vector.tensor_reduce(out=sum_b[:], in_=flat(part_b[:]), axis=AXIS.X, op=ALU.add)
 
-        for g in range(GROUPS - DEFER_GROUPS, GROUPS):
+        for g in range(GROUPS):
             mx_pass("c_a", g)
         part_a = soft.tile([P, BATCH, BLOCKS, BLOCK], F32, name="part_a")
         nc.vector.tensor_tensor(

@@ -18,26 +18,22 @@ PACK = 4
 K_PASS = P * PACK
 BATCH, SEQ, DIM, FEAT, BLOCK = 2, 256, 16384, 128, 4
 TOKENS = BATCH * SEQ
-TOKEN_TILES = TOKENS // P
 GROUPS = DIM // K_PASS
 BLOCKS = SEQ // BLOCK
 WINDOW = 2 * BLOCK
 GROUP_BLOCKS = K_PASS // 32
-PAIRS = K_PASS // 2
 
 CHUNK_GROUPS = 4
 CHUNKS = GROUPS // CHUNK_GROUPS
 CHUNK_K = CHUNK_GROUPS * K_PASS
-RAW_BUFS = 3
-ROUND_GROUPS = 2
-ROUNDS = GROUPS // ROUND_GROUPS
-ROUNDS_PER_CHUNK = CHUNK_GROUPS // ROUND_GROUPS
+RAW_BUFS = 6
+SEQ_TILES = SEQ // P
+ROUNDS = CHUNKS * BATCH
 
 LOGITS = ("z_a", "z_b")
 VALUES = ("c_b", "c_a")
 PROJECTIONS = LOGITS + VALUES
 STREAMED = LOGITS + ("c_b",)
-FIRST_SPLIT = 2
 BIAS_CHUNK = 2
 NEG = -3.4028234663852886e38
 
@@ -60,7 +56,6 @@ def tile_tokenlevelcompressor_pa_k_kernel(
     out,
 ):
     nc = tc.nc
-    h_rows = h.rearrange("b s d -> (b s) d")
     words_in = {"z_a": w_z_a_words, "z_b": w_z_b_words, "c_b": w_kv_b_words, "c_a": w_kv_a_words}
     scales_in = {"z_a": w_z_a_scales, "z_b": w_z_b_scales, "c_b": w_kv_b_scales, "c_a": w_kv_a_scales}
     plane_start = {"z_a": 0, "z_b": PACK, "c_b": 0, "c_a": 0}
@@ -69,7 +64,7 @@ def tile_tokenlevelcompressor_pa_k_kernel(
         ctx.enter_context(tc.manual_schedule())
         keep = ctx.enter_context(tc.tile_pool(name="keep", bufs=1))
         psum_acc = ctx.enter_context(tc.psum_pool(name="psum_acc", bufs=1))
-        psum_tr = ctx.enter_context(tc.psum_pool(name="psum_tr", bufs=4))
+        psum_tr = ctx.enter_context(tc.psum_pool(name="psum_tr", bufs=5))
 
         w_words = {n: keep.tile([P, GROUPS, FEAT], I32, name="w_words_" + n, align_bytes=64) for n in PROJECTIONS}
         logit_planes = keep.tile([P, GROUPS, FEAT], U8, name="logit_planes", align_bytes=64)
@@ -78,7 +73,7 @@ def tile_tokenlevelcompressor_pa_k_kernel(
             w_planes[n] = keep.tile([P, GROUPS, FEAT], U8, name="planes_" + n, align_bytes=64)
         h_codes = keep.tile([P, GROUPS, TOKENS], U32, name="h_codes", align_bytes=64)
         h_planes = keep.tile([P, GROUPS, TOKENS], U8, name="h_planes", align_bytes=64)
-        acc = {n: psum_acc.tile([P, TOKENS], F32, name="acc_" + n) for n in PROJECTIONS}
+        acc = {n: psum_acc.tile([P, TOKENS], F32, name="acc_" + n) for n in STREAMED}
 
         def load_words(name, c):
             groups = slice(c * CHUNK_GROUPS, (c + 1) * CHUNK_GROUPS)
@@ -95,13 +90,13 @@ def tile_tokenlevelcompressor_pa_k_kernel(
                     in_=rows[s : GROUP_BLOCKS : PACK],
                 )
 
-        def mx_pass(name, g):
+        def mx_pass(out, name, g, tokens):
             nc.tensor.matmul_mx(
-                out=acc[name][:],
+                out=out,
                 lhsT=w_words[name][:, g, :].bitcast(FP8X4),
                 lhsT_scale=w_planes[name][plane_start[name] : P, g, :],
-                rhs=h_codes[:, g, :].bitcast(FP8X4),
-                rhs_scale=h_planes[:, g, :],
+                rhs=h_codes[:, g, tokens].bitcast(FP8X4),
+                rhs_scale=h_planes[:, g, tokens],
                 start=(g == 0),
                 stop=(g == GROUPS - 1),
             )
@@ -125,86 +120,93 @@ def tile_tokenlevelcompressor_pa_k_kernel(
             nc.scalar.copy(out=bias[:], in_=bias_bank[:, 0, 0:WINDOW])
 
         with tc.tile_pool(name="raw", bufs=RAW_BUFS) as raw_pool, tc.tile_pool(
-            name="sorted", bufs=2 * ROUND_GROUPS
-        ) as sorted_pool, tc.tile_pool(name="grouped", bufs=3) as grouped_pool:
+            name="sorted", bufs=2
+        ) as sorted_pool, tc.tile_pool(name="grouped", bufs=6) as grouped_pool:
             raw_of = {}
             sorted_of = {}
             grouped_of = {}
 
-            def load_h(c):
-                raw = raw_pool.tile([P, TOKEN_TILES, CHUNK_K], BF16, name="raw")
-                step = FIRST_SPLIT * K_PASS if c == 0 else CHUNK_K
-                for k in range(0, CHUNK_K, step):
-                    nc.sync.dma_start(
-                        out=raw[:, :, k : k + step],
-                        in_=h_rows[:, c * CHUNK_K + k : c * CHUNK_K + k + step].rearrange("(t p) k -> p t k", p=P),
-                    )
-                raw_of[c] = raw
+            def load_h(r):
+                c, n = divmod(r, BATCH)
+                raw = raw_pool.tile([P, SEQ_TILES, CHUNK_K], BF16, name="raw")
+                nc.sync.dma_start(
+                    out=raw[:],
+                    in_=h[n, :, c * CHUNK_K : (c + 1) * CHUNK_K].rearrange("(t p) k -> p t k", p=P),
+                )
+                raw_of[r] = raw
 
-            def load_chunk(c):
-                load_h(c)
-                for name in STREAMED:
-                    load_words(name, c)
-                if c == BIAS_CHUNK:
-                    load_bias()
-                if c == CHUNKS - 1:
-                    load_scales("c_a")
-                    for other in range(CHUNKS):
-                        load_words("c_a", other)
+            def load_round(r):
+                c, n = divmod(r, BATCH)
+                load_h(r)
+                if n == BATCH - 1:
+                    for name in STREAMED:
+                        load_words(name, c)
+                    if c == BIAS_CHUNK:
+                        load_bias()
+                    if c == CHUNKS - 1:
+                        load_scales("c_a")
+                        for other in range(CHUNKS):
+                            load_words("c_a", other)
 
             def sort_round(r):
-                for g in range(r * ROUND_GROUPS, (r + 1) * ROUND_GROUPS):
-                    raw_words = raw_of[g // CHUNK_GROUPS][:].bitcast(F32)
-                    first = (g % CHUNK_GROUPS) * PAIRS
-                    sorted_words = sorted_pool.tile([P, TOKEN_TILES, 2, P], F32, name="sorted_words")
-                    nc.vector.tensor_copy(
-                        out=sorted_words[:],
-                        in_=raw_words[:, :, first : first + PAIRS].rearrange("p t (q u) -> p t u q", u=2),
-                    )
-                    sorted_of[g] = sorted_words
-                c = r // ROUNDS_PER_CHUNK
-                if r % ROUNDS_PER_CHUNK == ROUNDS_PER_CHUNK - 1 and c + RAW_BUFS < CHUNKS:
-                    load_chunk(c + RAW_BUFS)
+                sorted_words = sorted_pool.tile([P, SEQ_TILES, 2, CHUNK_GROUPS * P], F32, name="sorted_words")
+                raw_words = raw_of[r][:].bitcast(F32).rearrange("p t (q u) -> p t u q", u=2)
+                for half in range(2):
+                    columns = slice(half * CHUNK_GROUPS * P // 2, (half + 1) * CHUNK_GROUPS * P // 2)
+                    nc.vector.tensor_copy(out=sorted_words[:, :, :, columns], in_=raw_words[:, :, :, columns])
+                sorted_of[r] = sorted_words
+                if r + RAW_BUFS < ROUNDS:
+                    load_round(r + RAW_BUFS)
 
             def transpose_round(r):
-                for g in range(r * ROUND_GROUPS, (r + 1) * ROUND_GROUPS):
-                    grouped = grouped_pool.tile([P, TOKENS * PACK], BF16, name="grouped", align_bytes=64)
-                    grouped_words = grouped[:].bitcast(F32).rearrange("p (r u) -> p r u", u=2)
-                    for half in range(2):
-                        bank = psum_tr.tile([P, 2, 2 * P], F32, name="bank")
-                        for t in range(2):
-                            for u in range(2):
-                                nc.tensor.transpose(
-                                    bank[:, u, t * P : (t + 1) * P],
-                                    sorted_of[g][:, 2 * half + t, u, :],
-                                    ident[:],
-                                )
-                        nc.scalar.copy(
-                            out=grouped_words[:, half * 2 * P : (half + 1) * 2 * P, :],
-                            in_=bank[:].rearrange("p u r -> p r u"),
-                        )
-                    grouped_of[g] = grouped
+                for slot in range(CHUNK_GROUPS):
+                    bank = psum_tr.tile([P, 2, 2 * P], F32, name="bank")
+                    for t in range(SEQ_TILES):
+                        for u in range(2):
+                            nc.tensor.transpose(
+                                bank[:, u, t * P : (t + 1) * P],
+                                sorted_of[r][:, t, u, slot * P : (slot + 1) * P],
+                                ident[:],
+                            )
+                    grouped = grouped_pool.tile([P, SEQ * PACK], BF16, name="grouped", align_bytes=64)
+                    nc.scalar.copy(
+                        out=grouped[:].bitcast(F32).rearrange("p (r u) -> p r u", u=2),
+                        in_=bank[:].rearrange("p u r -> p r u"),
+                    )
+                    grouped_of[r, slot] = grouped
 
             def quantise_round(r):
-                for g in range(r * ROUND_GROUPS, (r + 1) * ROUND_GROUPS):
+                c, n = divmod(r, BATCH)
+                tokens = slice(n * SEQ, (n + 1) * SEQ)
+                for slot in range(CHUNK_GROUPS):
+                    g = c * CHUNK_GROUPS + slot
                     nc.vector.quantize_mx(
-                        out=h_codes[:, g, :].bitcast(FP8X4), scales=h_planes[:, g, :], in_=grouped_of[g][:]
+                        out=h_codes[:, g, tokens].bitcast(FP8X4),
+                        scales=h_planes[:, g, tokens],
+                        in_=grouped_of[r, slot][:],
                     )
 
+            def multiply(groups):
+                for name in STREAMED:
+                    for g in groups:
+                        mx_pass(acc[name][:], name, g, slice(0, TOKENS))
+
             load_h(0)
+            load_h(1)
             for name in LOGITS:
                 load_scales(name)
             for name in LOGITS:
                 load_words(name, 0)
             load_scales("c_b")
             load_words("c_b", 0)
-            for c in range(1, RAW_BUFS):
-                load_chunk(c)
+            for r in range(2, RAW_BUFS):
+                load_round(r)
 
             sort_round(0)
             sort_round(1)
             transpose_round(0)
             for r in range(ROUNDS):
+                c, n = divmod(r, BATCH)
                 if r == ROUNDS - 2:
                     nc.vector.tensor_copy(out=bias_rows[:], in_=bias_rows_bf[:])
                 quantise_round(r)
@@ -214,71 +216,89 @@ def tile_tokenlevelcompressor_pa_k_kernel(
                     transpose_round(r + 1)
                 if r == ROUNDS - 2:
                     transpose_bias()
-                for g in range(r * ROUND_GROUPS, (r + 1) * ROUND_GROUPS):
-                    for name in STREAMED:
-                        mx_pass(name, g)
+                if n == 1:
+                    multiply(range(c * CHUNK_GROUPS, c * CHUNK_GROUPS + CHUNK_GROUPS // 2))
+                elif c > 0:
+                    multiply(range(c * CHUNK_GROUPS - CHUNK_GROUPS // 2, c * CHUNK_GROUPS))
+            multiply(range(GROUPS - CHUNK_GROUPS // 2, GROUPS))
 
         soft = ctx.enter_context(tc.tile_pool(name="soft", bufs=1))
 
         def by_block(ap):
-            return ap.rearrange("p (n j i) -> p n j i", n=BATCH, i=BLOCK)
-
-        def flat(ap):
-            return ap.rearrange("p n j e -> p (n j) e")
+            return ap.rearrange("p (j i) -> p j i", i=BLOCK)
 
         window = soft.tile([P, BATCH, BLOCKS, WINDOW], F32, name="window")
-        nc.vector.memset(window[:, :, 0:1, 0:BLOCK], NEG)
-        nc.vector.tensor_tensor(
-            out=window[:, :, 1:BLOCKS, 0:BLOCK],
-            in0=by_block(acc["z_b"][:])[:, :, 0 : BLOCKS - 1, :],
-            in1=bias[:, 0:BLOCK].unsqueeze(1).unsqueeze(1).to_broadcast([P, BATCH, BLOCKS - 1, BLOCK]),
-            op=ALU.add,
-        )
-        nc.vector.tensor_tensor(
-            out=window[:, :, :, BLOCK:WINDOW],
-            in0=by_block(acc["z_a"][:]),
-            in1=bias[:, BLOCK:WINDOW].unsqueeze(1).unsqueeze(1).to_broadcast([P, BATCH, BLOCKS, BLOCK]),
-            op=ALU.add,
-        )
-        top_logit = soft.tile([P, BATCH * BLOCKS], F32, name="top_logit")
-        nc.vector.tensor_reduce(out=top_logit[:], in_=flat(window[:]), axis=AXIS.X, op=ALU.max)
-        nc.vector.tensor_tensor(
-            out=flat(window[:]),
-            in0=flat(window[:]),
-            in1=top_logit[:].unsqueeze(2).to_broadcast([P, BATCH * BLOCKS, WINDOW]),
-            op=ALU.subtract,
-        )
+        top_logit = soft.tile([P, BATCH, BLOCKS], F32, name="top_logit")
         weight = soft.tile([P, BATCH, BLOCKS, WINDOW], F32, name="weight")
-        nc.scalar.activation(out=flat(weight[:]), in_=flat(window[:]), func=ACT.Exp)
-        total = soft.tile([P, BATCH * BLOCKS], F32, name="total")
-        nc.vector.tensor_reduce(out=total[:], in_=flat(weight[:]), axis=AXIS.X, op=ALU.add)
-        inverse = soft.tile([P, BATCH * BLOCKS], F32, name="inverse")
-        nc.vector.reciprocal(out=inverse[:], in_=total[:])
+        total = soft.tile([P, BATCH, BLOCKS], F32, name="total")
+        inverse = soft.tile([P, BATCH, BLOCKS], F32, name="inverse")
+        nc.vector.memset(window[:, :, 0:1, 0:BLOCK], NEG)
+        seqs = range(BATCH)
+        for n in seqs:
+            tokens = slice(n * SEQ, (n + 1) * SEQ)
+            nc.vector.tensor_tensor(
+                out=window[:, n, 1:BLOCKS, 0:BLOCK],
+                in0=by_block(acc["z_b"][:, tokens])[:, 0 : BLOCKS - 1, :],
+                in1=bias[:, 0:BLOCK].unsqueeze(1).to_broadcast([P, BLOCKS - 1, BLOCK]),
+                op=ALU.add,
+            )
+            nc.vector.tensor_tensor(
+                out=window[:, n, :, BLOCK:WINDOW],
+                in0=by_block(acc["z_a"][:, tokens]),
+                in1=bias[:, BLOCK:WINDOW].unsqueeze(1).to_broadcast([P, BLOCKS, BLOCK]),
+                op=ALU.add,
+            )
+        for n in seqs:
+            nc.vector.tensor_reduce(out=top_logit[:, n, :], in_=window[:, n], axis=AXIS.X, op=ALU.max)
+        for n in seqs:
+            nc.vector.tensor_tensor(
+                out=window[:, n],
+                in0=window[:, n],
+                in1=top_logit[:, n, :].unsqueeze(2).to_broadcast([P, BLOCKS, WINDOW]),
+                op=ALU.subtract,
+            )
+            nc.scalar.activation(out=weight[:, n], in_=window[:, n], func=ACT.Exp)
+        for n in seqs:
+            nc.vector.tensor_reduce(out=total[:, n, :], in_=weight[:, n], axis=AXIS.X, op=ALU.add)
 
         part_b = soft.tile([P, BATCH, BLOCKS, BLOCK], F32, name="part_b")
         nc.vector.memset(part_b[:, :, 0:1, :], 0.0)
         nc.vector.tensor_tensor(
             out=part_b[:, :, 1:BLOCKS, :],
             in0=weight[:, :, 1:BLOCKS, 0:BLOCK],
-            in1=by_block(acc["c_b"][:])[:, :, 0 : BLOCKS - 1, :],
+            in1=acc["c_b"][:].rearrange("p (n j i) -> p n j i", n=BATCH, i=BLOCK)[:, :, 0 : BLOCKS - 1, :],
             op=ALU.mult,
         )
-        sum_b = soft.tile([P, BATCH * BLOCKS], F32, name="sum_b")
-        nc.vector.tensor_reduce(out=sum_b[:], in_=flat(part_b[:]), axis=AXIS.X, op=ALU.add)
+        nc.vector.reciprocal(out=inverse[:], in_=total[:])
+        sum_b = soft.tile([P, BATCH, BLOCKS], F32, name="sum_b")
+        nc.vector.tensor_reduce(out=sum_b[:], in_=part_b[:], axis=AXIS.X, op=ALU.add)
 
-        for g in range(GROUPS):
-            mx_pass("c_a", g)
-        part_a = soft.tile([P, BATCH, BLOCKS, BLOCK], F32, name="part_a")
+        share_a = soft.tile([P, BATCH, BLOCKS, BLOCK], F32, name="share_a")
         nc.vector.tensor_tensor(
-            out=part_a[:], in0=weight[:, :, :, BLOCK:WINDOW], in1=by_block(acc["c_a"][:]), op=ALU.mult
+            out=share_a[:],
+            in0=weight[:, :, :, BLOCK:WINDOW],
+            in1=inverse[:].unsqueeze(3).to_broadcast([P, BATCH, BLOCKS, BLOCK]),
+            op=ALU.mult,
         )
-        result = soft.tile([P, BATCH * BLOCKS], F32, name="result")
-        nc.vector.tensor_reduce(out=result[:], in_=flat(part_a[:]), axis=AXIS.X, op=ALU.add)
-        nc.vector.tensor_tensor(out=result[:], in0=result[:], in1=sum_b[:], op=ALU.add)
-        nc.vector.tensor_tensor(out=result[:], in0=result[:], in1=inverse[:], op=ALU.mult)
+        nc.vector.tensor_tensor(out=sum_b[:], in0=sum_b[:], in1=inverse[:], op=ALU.mult)
+
+        c_a = [psum_tr.tile([P, 2, 2 * P], F32, name="bank") for n in range(BATCH)]
+        for run in range(2):
+            for n in range(BATCH):
+                for g in range(run * GROUPS // 2, (run + 1) * GROUPS // 2):
+                    mx_pass(c_a[n][:, 0, :], "c_a", g, slice(n * SEQ, (n + 1) * SEQ))
+        result = soft.tile([P, BATCH, BLOCKS], F32, name="result")
+        for n in range(BATCH):
+            part_a = soft.tile([P, BLOCKS, BLOCK], F32, name="part_a")
+            nc.vector.tensor_tensor(
+                out=part_a[:], in0=share_a[:, n], in1=by_block(c_a[n][:, 0, :]), op=ALU.mult
+            )
+            sum_a = soft.tile([P, BLOCKS], F32, name="sum_a")
+            nc.vector.tensor_reduce(out=sum_a[:], in_=part_a[:], axis=AXIS.X, op=ALU.add)
+            nc.vector.tensor_tensor(out=result[:, n, :], in0=sum_a[:], in1=sum_b[:, n, :], op=ALU.add)
 
         result_bank = psum_tr.tile([P, 2, 2 * P], F32, name="bank")
-        nc.tensor.transpose(result_bank[:, 0, 0:P], result[:], ident[:])
+        nc.tensor.transpose(result_bank[:, 0, 0:P], result[:].rearrange("p n j -> p (n j)"), ident[:])
         result_rows = soft.tile([P, FEAT], F32, name="result_rows")
         nc.vector.tensor_copy(out=result_rows[:], in_=result_bank[:, 0, 0:P])
         nc.sync.dma_start(out=out.rearrange("n j f -> (n j) f"), in_=result_rows[:])

@@ -28,13 +28,14 @@ CHUNKS = GROUPS // CHUNK_GROUPS
 CHUNK_K = CHUNK_GROUPS * K_PASS
 RAW_BUFS = 6
 SEQ_TILES = SEQ // P
+BIAS_ROUND = 5
+STEP_GROUPS = CHUNK_GROUPS // BATCH
 ROUNDS = CHUNKS * BATCH
 
 LOGITS = ("z_a", "z_b")
 VALUES = ("c_b", "c_a")
 PROJECTIONS = LOGITS + VALUES
 STREAMED = LOGITS + ("c_b",)
-BIAS_CHUNK = 2
 NEG = -3.4028234663852886e38
 
 FLOPS = 2 * TOKENS * DIM * len(PROJECTIONS) * FEAT
@@ -138,15 +139,21 @@ def tile_tokenlevelcompressor_pa_k_kernel(
             def load_round(r):
                 c, n = divmod(r, BATCH)
                 load_h(r)
-                if n == BATCH - 1:
+                if n == 0:
+                    for name in LOGITS:
+                        load_words(name, c - 1)
+                else:
+                    load_words("c_b", c - 1)
+                if r == BATCH + 1:
+                    load_scales("c_b")
+                if r == BIAS_ROUND:
+                    load_bias()
+                if r == ROUNDS - 1:
                     for name in STREAMED:
                         load_words(name, c)
-                    if c == BIAS_CHUNK:
-                        load_bias()
-                    if c == CHUNKS - 1:
-                        load_scales("c_a")
-                        for other in range(CHUNKS):
-                            load_words("c_a", other)
+                    load_scales("c_a")
+                    for other in range(CHUNKS):
+                        load_words("c_a", other)
 
             def sort_round(r):
                 sorted_words = sorted_pool.tile([P, SEQ_TILES, 2, CHUNK_GROUPS * P], F32, name="sorted_words")
@@ -186,20 +193,16 @@ def tile_tokenlevelcompressor_pa_k_kernel(
                         in_=grouped_of[r, slot][:],
                     )
 
-            def multiply(groups):
-                for name in STREAMED:
-                    for g in groups:
+            def multiply(names, step):
+                for name in names:
+                    for g in range(step * STEP_GROUPS, (step + 1) * STEP_GROUPS):
                         mx_pass(acc[name][:], name, g, slice(0, TOKENS))
 
-            load_h(0)
-            load_h(1)
+            for r in range(BATCH):
+                load_h(r)
             for name in LOGITS:
                 load_scales(name)
-            for name in LOGITS:
-                load_words(name, 0)
-            load_scales("c_b")
-            load_words("c_b", 0)
-            for r in range(2, RAW_BUFS):
+            for r in range(BATCH, RAW_BUFS):
                 load_round(r)
 
             sort_round(0)
@@ -216,11 +219,13 @@ def tile_tokenlevelcompressor_pa_k_kernel(
                     transpose_round(r + 1)
                 if r == ROUNDS - 2:
                     transpose_bias()
-                if n == 1:
-                    multiply(range(c * CHUNK_GROUPS, c * CHUNK_GROUPS + CHUNK_GROUPS // 2))
-                elif c > 0:
-                    multiply(range(c * CHUNK_GROUPS - CHUNK_GROUPS // 2, c * CHUNK_GROUPS))
-            multiply(range(GROUPS - CHUNK_GROUPS // 2, GROUPS))
+                if r > 0:
+                    multiply(LOGITS, r - 1)
+                if r > BATCH:
+                    multiply(("c_b",), r - 1 - BATCH)
+            multiply(LOGITS, ROUNDS - 1)
+            for step in range(ROUNDS - 1 - BATCH, ROUNDS):
+                multiply(("c_b",), step)
 
         soft = ctx.enter_context(tc.tile_pool(name="soft", bufs=1))
 

@@ -35,7 +35,6 @@ ROUNDS = CHUNKS * BATCH
 LOGITS = ("z_a", "z_b")
 VALUES = ("c_b", "c_a")
 PROJECTIONS = LOGITS + VALUES
-STREAMED = LOGITS + ("c_b",)
 NEG = -3.4028234663852886e38
 
 FLOPS = 2 * TOKENS * DIM * len(PROJECTIONS) * FEAT
@@ -74,7 +73,7 @@ def tile_tokenlevelcompressor_pa_k_kernel(
             w_planes[n] = keep.tile([P, GROUPS, FEAT], U8, name="planes_" + n, align_bytes=64)
         h_codes = keep.tile([P, GROUPS, TOKENS], U32, name="h_codes", align_bytes=64)
         h_planes = keep.tile([P, GROUPS, TOKENS], U8, name="h_planes", align_bytes=64)
-        acc = {n: psum_acc.tile([P, TOKENS], F32, name="acc_" + n) for n in STREAMED}
+        acc = {n: psum_acc.tile([P, TOKENS], F32, name="acc_" + n) for n in LOGITS + ("c_b",)}
 
         def load_words(name, c):
             groups = slice(c * CHUNK_GROUPS, (c + 1) * CHUNK_GROUPS)
@@ -142,18 +141,15 @@ def tile_tokenlevelcompressor_pa_k_kernel(
                 if n == 0:
                     for name in LOGITS:
                         load_words(name, c - 1)
-                else:
-                    load_words("c_b", c - 1)
-                if r == BATCH + 1:
-                    load_scales("c_b")
                 if r == BIAS_ROUND:
                     load_bias()
                 if r == ROUNDS - 1:
-                    for name in STREAMED:
+                    for name in LOGITS:
                         load_words(name, c)
-                    load_scales("c_a")
-                    for other in range(CHUNKS):
-                        load_words("c_a", other)
+                    for name in VALUES:
+                        load_scales(name)
+                        for other in range(CHUNKS):
+                            load_words(name, other)
 
             def sort_round(r):
                 sorted_words = sorted_pool.tile([P, SEQ_TILES, 2, CHUNK_GROUPS * P], F32, name="sorted_words")
@@ -221,10 +217,8 @@ def tile_tokenlevelcompressor_pa_k_kernel(
                     transpose_bias()
                 if r > 0:
                     multiply(LOGITS, r - 1)
-                if r > BATCH:
-                    multiply(("c_b",), r - 1 - BATCH)
             multiply(LOGITS, ROUNDS - 1)
-            for step in range(ROUNDS - 1 - BATCH, ROUNDS):
+            for step in range(ROUNDS):
                 multiply(("c_b",), step)
 
         soft = ctx.enter_context(tc.tile_pool(name="soft", bufs=1))

@@ -129,10 +129,12 @@ def tile_tokenlevelcompressor_pa_k_kernel(
             def load_h(r):
                 c, n = divmod(r, BATCH)
                 raw = raw_pool.tile([P, SEQ_TILES, CHUNK_K], BF16, name="raw")
-                nc.sync.dma_start(
-                    out=raw[:],
-                    in_=h[n, :, c * CHUNK_K : (c + 1) * CHUNK_K].rearrange("(t p) k -> p t k", p=P),
-                )
+                part = CHUNK_K // 2 if r == ROUNDS - 1 else CHUNK_K
+                for k in range(0, CHUNK_K, part):
+                    nc.sync.dma_start(
+                        out=raw[:, :, k : k + part],
+                        in_=h[n, :, c * CHUNK_K + k : c * CHUNK_K + k + part].rearrange("(t p) k -> p t k", p=P),
+                    )
                 raw_of[r] = raw
 
             def load_round(r):
@@ -282,10 +284,13 @@ def tile_tokenlevelcompressor_pa_k_kernel(
         nc.vector.tensor_tensor(out=sum_b[:], in0=sum_b[:], in1=inverse[:], op=ALU.mult)
 
         c_a = [psum_tr.tile([P, 2, 2 * P], F32, name="bank") for n in range(BATCH)]
-        for run in range(2):
+        for c in range(CHUNKS // 2):
             for n in range(BATCH):
-                for g in range(run * GROUPS // 2, (run + 1) * GROUPS // 2):
+                for g in range(c * CHUNK_GROUPS, (c + 1) * CHUNK_GROUPS):
                     mx_pass(c_a[n][:, 0, :], "c_a", g, slice(n * SEQ, (n + 1) * SEQ))
+        for n in range(BATCH):
+            for g in range(GROUPS // 2, GROUPS):
+                mx_pass(c_a[n][:, 0, :], "c_a", g, slice(n * SEQ, (n + 1) * SEQ))
         result = soft.tile([P, BATCH, BLOCKS], F32, name="result")
         for n in range(BATCH):
             part_a = soft.tile([P, BLOCKS, BLOCK], F32, name="part_a")

from contextlib import ExitStack

import concourse.mybir as mybir
from concourse.masks import make_identity

F32 = mybir.dt.float32
BF16 = mybir.dt.bfloat16
I32 = mybir.dt.int32
U32 = mybir.dt.uint32
U8 = mybir.dt.uint8
FP8X4 = mybir.dt.float8_e4m3fn_x4
ALU = mybir.AluOpType
ACT = mybir.ActivationFunctionType
AXIS = mybir.AxisListType

P = 128
PACK = 4
K_PASS = P * PACK
BATCH, SEQ, DIM, FEAT, BLOCK = 2, 256, 16384, 128, 4
TOKENS = BATCH * SEQ
GROUPS = DIM // K_PASS
BLOCKS = SEQ // BLOCK
WINDOW = 2 * BLOCK
GROUP_BLOCKS = K_PASS // 32

CHUNK_GROUPS = 4
CHUNKS = GROUPS // CHUNK_GROUPS
CHUNK_K = CHUNK_GROUPS * K_PASS
RAW_BUFS = 6
SEQ_TILES = SEQ // P
BIAS_ROUND = 5
STEP_GROUPS = CHUNK_GROUPS // BATCH
ROUNDS = CHUNKS * BATCH

LOGITS = ("z_a", "z_b")
VALUES = ("c_b", "c_a")
PROJECTIONS = LOGITS + VALUES
NEG = -3.4028234663852886e38

FLOPS = 2 * TOKENS * DIM * len(PROJECTIONS) * FEAT


def tile_tokenlevelcompressor_pa_k_kernel(
    tc,
    h,
    w_kv_a_words,
    w_kv_a_scales,
    w_kv_b_words,
    w_kv_b_scales,
    w_z_a_words,
    w_z_a_scales,
    w_z_b_words,
    w_z_b_scales,
    b_a,
    b_b,
    out,
):
    nc = tc.nc
    words_in = {"z_a": w_z_a_words, "z_b": w_z_b_words, "c_b": w_kv_b_words, "c_a": w_kv_a_words}
    scales_in = {"z_a": w_z_a_scales, "z_b": w_z_b_scales, "c_b": w_kv_b_scales, "c_a": w_kv_a_scales}
    plane_start = {"z_a": 0, "z_b": PACK, "c_b": 0, "c_a": 0}

    with ExitStack() as ctx:
        ctx.enter_context(tc.manual_schedule())
        keep = ctx.enter_context(tc.tile_pool(name="keep", bufs=1))
        psum_acc = ctx.enter_context(tc.psum_pool(name="psum_acc", bufs=1))
        psum_tr = ctx.enter_context(tc.psum_pool(name="psum_tr", bufs=5))

        w_words = {n: keep.tile([P, GROUPS, FEAT], I32, name="w_words_" + n, align_bytes=64) for n in PROJECTIONS}
        logit_planes = keep.tile([P, GROUPS, FEAT], U8, name="logit_planes", align_bytes=64)
        w_planes = {n: logit_planes for n in LOGITS}
        for n in VALUES:
            w_planes[n] = keep.tile([P, GROUPS, FEAT], U8, name="planes_" + n, align_bytes=64)
        h_codes = keep.tile([P, GROUPS, TOKENS], U32, name="h_codes", align_bytes=64)
        h_planes = keep.tile([P, GROUPS, TOKENS], U8, name="h_planes", align_bytes=64)
        acc = {n: psum_acc.tile([P, TOKENS], F32, name="acc_" + n) for n in LOGITS + ("c_b",)}

        def load_words(name, c):
            groups = slice(c * CHUNK_GROUPS, (c + 1) * CHUNK_GROUPS)
            nc.sync.dma_start(
                out=w_words[name][:, groups, :],
                in_=words_in[name][groups].rearrange("g p n t -> p g (n t)").bitcast(I32),
            )

        def load_scales(name):
            rows = scales_in[name].rearrange("g q n -> q g n").bitcast(I32)
            for s in range(PACK):
                nc.sync.dma_start(
                    out=w_planes[name][plane_start[name] + s : P : 32, :, :].bitcast(I32),
                    in_=rows[s : GROUP_BLOCKS : PACK],
                )

        def mx_pass(out, name, g, tokens):
            nc.tensor.matmul_mx(
                out=out,
                lhsT=w_words[name][:, g, :].bitcast(FP8X4),
                lhsT_scale=w_planes[name][plane_start[name] : P, g, :],
                rhs=h_codes[:, g, tokens].bitcast(FP8X4),
                rhs_scale=h_planes[:, g, tokens],
                start=(g == 0),
                stop=(g == GROUPS - 1),
            )

        ident = keep.tile([P, P], F32, name="ident")
        make_identity(nc, ident[:])
        for planes in (logit_planes, w_planes["c_b"], w_planes["c_a"]):
            nc.vector.memset(planes[:].rearrange("p g n -> p (g n)").bitcast(I32), 0)
        bias_rows_bf = keep.tile([P, P], BF16, name="bias_rows_bf")
        nc.vector.memset(bias_rows_bf[:], 0.0)
        bias_rows = keep.tile([P, P], F32, name="bias_rows")
        bias = keep.tile([P, WINDOW], F32, name="bias")

        def load_bias():
            nc.sync.dma_start(out=bias_rows_bf[0:BLOCK, :], in_=b_b)
            nc.sync.dma_start(out=bias_rows_bf[BLOCK:WINDOW, :], in_=b_a)

        def transpose_bias():
            bias_bank = psum_tr.tile([P, 2, 2 * P], F32, name="bank")
            nc.tensor.transpose(bias_bank[:, 0, 0:P], bias_rows[:], ident[:])
            nc.scalar.copy(out=bias[:], in_=bias_bank[:, 0, 0:WINDOW])

        with tc.tile_pool(name="raw", bufs=RAW_BUFS) as raw_pool, tc.tile_pool(
            name="sorted", bufs=2
        ) as sorted_pool, tc.tile_pool(name="grouped", bufs=6) as grouped_pool:
            raw_of = {}
            sorted_of = {}
            grouped_of = {}

            def load_h(r):
                c, n = divmod(r, BATCH)
                raw = raw_pool.tile([P, SEQ_TILES, CHUNK_K], BF16, name="raw")
                part = CHUNK_K // 2 if r == ROUNDS - 1 else CHUNK_K
                for k in range(0, CHUNK_K, part):
                    nc.sync.dma_start(
                        out=raw[:, :, k : k + part],
                        in_=h[n, :, c * CHUNK_K + k : c * CHUNK_K + k + part].rearrange("(t p) k -> p t k", p=P),
                    )
                raw_of[r] = raw

            def load_round(r):
                c, n = divmod(r, BATCH)
                load_h(r)
                if n == 0:
                    for name in LOGITS:
                        load_words(name, c - 1)
                if r == BIAS_ROUND:
                    load_bias()
                if r == ROUNDS - 1:
                    for name in LOGITS:
                        load_words(name, c)
                    for name in VALUES:
                        load_scales(name)
                        for other in range(CHUNKS):
                            load_words(name, other)

            def sort_round(r):
                sorted_words = sorted_pool.tile([P, SEQ_TILES, 2, CHUNK_GROUPS * P], F32, name="sorted_words")
                raw_words = raw_of[r][:].bitcast(F32).rearrange("p t (q u) -> p t u q", u=2)
                for half in range(2):
                    columns = slice(half * CHUNK_GROUPS * P // 2, (half + 1) * CHUNK_GROUPS * P // 2)
                    nc.vector.tensor_copy(out=sorted_words[:, :, :, columns], in_=raw_words[:, :, :, columns])
                sorted_of[r] = sorted_words
                if r + RAW_BUFS < ROUNDS:
                    load_round(r + RAW_BUFS)

            def transpose_round(r):
                for slot in range(CHUNK_GROUPS):
                    bank = psum_tr.tile([P, 2, 2 * P], F32, name="bank")
                    for t in range(SEQ_TILES):
                        for u in range(2):
                            nc.tensor.transpose(
                                bank[:, u, t * P : (t + 1) * P],
                                sorted_of[r][:, t, u, slot * P : (slot + 1) * P],
                                ident[:],
                            )
                    grouped = grouped_pool.tile([P, SEQ * PACK], BF16, name="grouped", align_bytes=64)
                    nc.scalar.copy(
                        out=grouped[:].bitcast(F32).rearrange("p (r u) -> p r u", u=2),
                        in_=bank[:].rearrange("p u r -> p r u"),
                    )
                    grouped_of[r, slot] = grouped

            def quantise_round(r):
                c, n = divmod(r, BATCH)
                tokens = slice(n * SEQ, (n + 1) * SEQ)
                for slot in range(CHUNK_GROUPS):
                    g = c * CHUNK_GROUPS + slot
                    nc.vector.quantize_mx(
                        out=h_codes[:, g, tokens].bitcast(FP8X4),
                        scales=h_planes[:, g, tokens],
                        in_=grouped_of[r, slot][:],
                    )

            def multiply(names, step):
                for name in names:
                    for g in range(step * STEP_GROUPS, (step + 1) * STEP_GROUPS):
                        mx_pass(acc[name][:], name, g, slice(0, TOKENS))

            for r in range(BATCH):
                load_h(r)
            for name in LOGITS:
                load_scales(name)
            for r in range(BATCH, RAW_BUFS):
                load_round(r)

            sort_round(0)
            sort_round(1)
            transpose_round(0)
            for r in range(ROUNDS):
                c, n = divmod(r, BATCH)
                if r == ROUNDS - 2:
                    nc.vector.tensor_copy(out=bias_rows[:], in_=bias_rows_bf[:])
                quantise_round(r)
                if r + 2 < ROUNDS:
                    sort_round(r + 2)
                if r + 1 < ROUNDS:
                    transpose_round(r + 1)
                if r == ROUNDS - 2:
                    transpose_bias()
                if r > 0:
                    multiply(LOGITS, r - 1)
            multiply(LOGITS, ROUNDS - 1)
            for step in range(ROUNDS):
                multiply(("c_b",), step)

        soft = ctx.enter_context(tc.tile_pool(name="soft", bufs=1))

        def by_block(ap):
            return ap.rearrange("p (j i) -> p j i", i=BLOCK)

        window = soft.tile([P, BATCH, BLOCKS, WINDOW], F32, name="window")
        top_logit = soft.tile([P, BATCH, BLOCKS], F32, name="top_logit")
        weight = soft.tile([P, BATCH, BLOCKS, WINDOW], F32, name="weight")
        total = soft.tile([P, BATCH, BLOCKS], F32, name="total")
        inverse = soft.tile([P, BATCH, BLOCKS], F32, name="inverse")
        nc.vector.memset(window[:, :, 0:1, 0:BLOCK], NEG)
        seqs = range(BATCH)
        for n in seqs:
            tokens = slice(n * SEQ, (n + 1) * SEQ)
            nc.vector.tensor_tensor(
                out=window[:, n, 1:BLOCKS, 0:BLOCK],
                in0=by_block(acc["z_b"][:, tokens])[:, 0 : BLOCKS - 1, :],
                in1=bias[:, 0:BLOCK].unsqueeze(1).to_broadcast([P, BLOCKS - 1, BLOCK]),
                op=ALU.add,
            )
            nc.vector.tensor_tensor(
                out=window[:, n, :, BLOCK:WINDOW],
                in0=by_block(acc["z_a"][:, tokens]),
                in1=bias[:, BLOCK:WINDOW].unsqueeze(1).to_broadcast([P, BLOCKS, BLOCK]),
                op=ALU.add,
            )
        for n in seqs:
            nc.vector.tensor_reduce(out=top_logit[:, n, :], in_=window[:, n], axis=AXIS.X, op=ALU.max)
        for n in seqs:
            nc.vector.tensor_tensor(
                out=window[:, n],
                in0=window[:, n],
                in1=top_logit[:, n, :].unsqueeze(2).to_broadcast([P, BLOCKS, WINDOW]),
                op=ALU.subtract,
            )
            nc.scalar.activation(out=weight[:, n], in_=window[:, n], func=ACT.Exp)
        for n in seqs:
            nc.vector.tensor_reduce(out=total[:, n, :], in_=weight[:, n], axis=AXIS.X, op=ALU.add)

        part_b = soft.tile([P, BATCH, BLOCKS, BLOCK], F32, name="part_b")
        nc.vector.memset(part_b[:, :, 0:1, :], 0.0)
        nc.vector.tensor_tensor(
            out=part_b[:, :, 1:BLOCKS, :],
            in0=weight[:, :, 1:BLOCKS, 0:BLOCK],
            in1=acc["c_b"][:].rearrange("p (n j i) -> p n j i", n=BATCH, i=BLOCK)[:, :, 0 : BLOCKS - 1, :],
            op=ALU.mult,
        )
        nc.vector.reciprocal(out=inverse[:], in_=total[:])
        sum_b = soft.tile([P, BATCH, BLOCKS], F32, name="sum_b")
        nc.vector.tensor_reduce(out=sum_b[:], in_=part_b[:], axis=AXIS.X, op=ALU.add)

        share_a = soft.tile([P, BATCH, BLOCKS, BLOCK], F32, name="share_a")
        nc.vector.tensor_tensor(
            out=share_a[:],
            in0=weight[:, :, :, BLOCK:WINDOW],
            in1=inverse[:].unsqueeze(3).to_broadcast([P, BATCH, BLOCKS, BLOCK]),
            op=ALU.mult,
        )
        nc.vector.tensor_tensor(out=sum_b[:], in0=sum_b[:], in1=inverse[:], op=ALU.mult)

        c_a = [psum_tr.tile([P, 2, 2 * P], F32, name="bank") for n in range(BATCH)]
        for c in range(CHUNKS // 2):
            for n in range(BATCH):
                for g in range(c * CHUNK_GROUPS, (c + 1) * CHUNK_GROUPS):
                    mx_pass(c_a[n][:, 0, :], "c_a", g, slice(n * SEQ, (n + 1) * SEQ))
        for n in range(BATCH):
            for g in range(GROUPS // 2, GROUPS):
                mx_pass(c_a[n][:, 0, :], "c_a", g, slice(n * SEQ, (n + 1) * SEQ))
        result = soft.tile([P, BATCH, BLOCKS], F32, name="result")
        for n in range(BATCH):
            part_a = soft.tile([P, BLOCKS, BLOCK], F32, name="part_a")
            nc.vector.tensor_tensor(
                out=part_a[:], in0=share_a[:, n], in1=by_block(c_a[n][:, 0, :]), op=ALU.mult
            )
            sum_a = soft.tile([P, BLOCKS], F32, name="sum_a")
            nc.vector.tensor_reduce(out=sum_a[:], in_=part_a[:], axis=AXIS.X, op=ALU.add)
            nc.vector.tensor_tensor(out=result[:, n, :], in0=sum_a[:], in1=sum_b[:, n, :], op=ALU.add)

        result_bank = psum_tr.tile([P, 2, 2 * P], F32, name="bank")
        nc.tensor.transpose(result_bank[:, 0, 0:P], result[:].rearrange("p n j -> p (n j)"), ident[:])
        result_rows = soft.tile([P, FEAT], F32, name="result_rows")
        nc.vector.tensor_copy(out=result_rows[:], in_=result_bank[:, 0, 0:P])
        nc.sync.dma_start(out=out.rearrange("n j f -> (n j) f"), in_=result_rows[:])
